import numpy as np
import ml_dtypes


def mxq(x, axis, fmt="e4m3"):
    dtype, down = {"e4m3": (ml_dtypes.float8_e4m3fn, 7), "e5m2": (ml_dtypes.float8_e5m2, 14)}[fmt]
    v = np.moveaxis(np.asarray(x, np.float32).astype(ml_dtypes.bfloat16).astype(np.float64), axis, -1)
    blocks = v.reshape(v.shape[:-1] + (-1, 32))
    amax = np.abs(blocks).max(-1, keepdims=True)
    byte = np.maximum(np.where(amax > 0, np.frexp(amax)[1] - 1 + 127, 0) - down, 1)
    scale = np.exp2(byte - 127.0)
    codes = (blocks / scale).astype(np.float32).astype(dtype).astype(np.float64)
    return np.moveaxis((codes * scale).reshape(v.shape), -1, axis)


WIDE = False


def mx_kscale(k):
    if not WIDE:
        return np.ones(k)
    levels = np.array([20, -20, 10, -10, 0])
    a = np.random.permutation(np.resize(levels, k // 512 * 4)).reshape(k // 512, 4)
    idx = np.arange(k)
    return np.exp2(a[idx // 512, idx % 128 // 32])


BF16 = ml_dtypes.bfloat16


def bf(x):
    return np.asarray(x, np.float32).astype(BF16)


def f64(x):
    return np.asarray(x).astype(np.float64)


LAG_IDXS = list(range(-10, 41))
NL = len(LAG_IDXS)
B, T = 2, 512
IN_DIM = 128
OUT_DIM = 512
REAL_IN_DIM = NL * IN_DIM


def time_lagging(x):
    nb, nt, nd = x.shape
    parts = []
    for lag in LAG_IDXS:
        if lag > 0:
            s = np.pad(x[:, : nt - lag], ((0, 0), (lag, 0), (0, 0)))
        elif lag < 0:
            s = np.pad(x[:, -lag:], ((0, 0), (0, -lag), (0, 0)))
        else:
            s = x
        parts.append(s)
    return np.concatenate(parts, axis=-1)


def setup_inputs():
    u = mx_kscale(OUT_DIM)
    x = np.random.standard_normal((B, T, IN_DIM))
    W = np.random.standard_normal((OUT_DIM, REAL_IN_DIM)) * (REAL_IN_DIM ** -0.5) / u[:, None]
    b = np.random.standard_normal(OUT_DIM) * 0.3
    g = np.random.standard_normal((B, T, OUT_DIM)) * np.exp2(np.random.randint(-12, 1, (B, T, 1))) * 4.0 * u
    return {"x": bf(x), "W": bf(W), "b": bf(b), "grad_out": bf(g)}


def reference(x, W, b, grad_out):
    glag = mxq(f64(grad_out), 2, "e5m2") @ mxq(f64(W), 0, "e4m3")
    glag = np.asarray(glag)
    out = np.zeros((B, T, IN_DIM))
    for l, lag in enumerate(LAG_IDXS):
        p = glag[:, :, l * IN_DIM:(l + 1) * IN_DIM]
        if lag > 0:
            out[:, : T - lag] += p[:, lag:]
        elif lag < 0:
            out[:, -lag:] += p[:, : T + lag]
        else:
            out += p
    return out

@@ -1,0 +1,245 @@
+from contextlib import ExitStack
+
+import concourse.mybir as mybir
+from concourse.masks import make_identity
+
+BF16 = mybir.dt.bfloat16
+F32 = mybir.dt.float32
+I32 = mybir.dt.int32
+U32 = mybir.dt.uint32
+U8 = mybir.dt.uint8
+E4X4 = mybir.dt.float8_e4m3fn_x4
+E5X4 = mybir.dt.float8_e5m2_x4
+
+P = 128
+NL = 51
+D = 128
+FLOPS = 2 * 1024 * 512 * NL * D
+BYTES = 512 * NL * D * 2 + 1024 * 512 * 2 + 1024 * D * 4
+
+NS = 16
+UPAD = 12
+NUU = 116
+ECOLS = NUU * NS
+
+CHUNKS = [(10, 2), (12, 2), (14, 4), (18, 4), (22, 4), (26, 4), (30, 4), (34, 4), (38, 4), (42, 4),
+          (46, 5), (0, 4), (4, 4), (8, 2)]
+
+
+def tile_ctrf_kernel(tc, x, W, b, grad_out, out):
+    nc = tc.nc
+    with ExitStack() as ctx:
+        keep = ctx.enter_context(tc.tile_pool(name="keep", bufs=1))
+        psum = ctx.enter_context(tc.psum_pool(name="psum", bufs=1))
+        ctx.enter_context(tc.manual_schedule())
+
+        g_view = grad_out.flatten_outer_dims().rearrange("(p r) o -> p r o", r=8)
+        out_view = out.flatten_outer_dims().rearrange("(p r) d -> p r d", r=8)
+        w_view = W.rearrange("(h q e) c -> h q e c", h=2, q=P, e=2)
+
+        ident = keep.tile([P, P], F32, name="ident")
+        make_identity(nc, ident[:])
+
+        e_bf = keep.tile([P, ECOLS * 4], BF16, name="e_bf", align_bytes=64)
+        e_codes = keep.tile([P, ECOLS], U32, name="e_codes", align_bytes=64)
+        planes = [keep.tile([P, ECOLS], U8, name="plane%d" % v, align_bytes=64) for v in range(4)]
+        e32 = e_bf[:].bitcast(F32)
+        e5d = e32.rearrange("p (uu g s h) -> p uu g s h", uu=NUU, g=2, s=8, h=2)
+        main = e32[:, 32 * UPAD:32 * (UPAD + 64)].rearrange(
+            "p (a r s h) -> p r a s h", a=8, r=8, s=NS, h=2)
+
+        nc.vector.memset(planes[0][:].bitcast(I32), 0)
+        nc.vector.memset(e32[:, 76 * 32:NUU * 32], 0.0)
+        nc.vector.memset(e32[:, 0:UPAD * 32], 0.0)
+
+        g_sb = keep.tile([P, 8, 512], BF16, name="g_sb")
+        raw = [keep.tile([P, 4, n * D], BF16, name="raw%d" % c) for c, (l0, n) in enumerate(CHUNKS)]
+        grp = [keep.tile([P, n * D, 4], BF16, name="grp%d" % c, align_bytes=64)
+               for c, (l0, n) in enumerate(CHUNKS)]
+        wcod = [keep.tile([P, n * D], U32, name="wcod%d" % c, align_bytes=64)
+                for c, (l0, n) in enumerate(CHUNKS)]
+        wsc = [keep.tile([P, n * D], U8, name="wsc%d" % c, align_bytes=64)
+               for c, (l0, n) in enumerate(CHUNKS)]
+
+        for i in range(4):
+            nc.sync.dma_start(out=g_sb[:, 2 * i:2 * i + 2, :], in_=g_view[:, 2 * i:2 * i + 2, :])
+        for c, (l0, n) in enumerate(CHUNKS):
+            for h in range(2):
+                nc.sync.dma_start(out=raw[c][:, 2 * h:2 * h + 2, :],
+                                  in_=w_view[h][:, :, l0 * D:(l0 + n) * D])
+
+        acc = [psum.tile([P, 512], F32, name="acc%d" % k) for k in range(2)]
+        g32 = g_sb[:].rearrange("p r o -> p (r o)").bitcast(F32)
+
+        def transpose_g(xt, j, r):
+            for h in range(2):
+                nc.tensor.transpose(xt[:, j, h, :], g32[:, r * 256 + h * P:r * 256 + (h + 1) * P],
+                                    ident[:])
+
+        def evac_g(eng, xt, j, r):
+            src = xt[:, j].rearrange("p h (s a) -> p a s h", s=NS, a=8)
+            if eng == "v":
+                nc.vector.tensor_copy(out=main[:, r], in_=src)
+            else:
+                nc.scalar.copy(out=main[:, r], in_=src)
+
+        def quant_g(c0, c1):
+            nc.vector.quantize_mx(out=e_codes[:, c0:c1].bitcast(E5X4), scales=planes[0][:, c0:c1],
+                                  in_=e_bf[:, 4 * c0:4 * c1])
+
+        def move(v, c0, c1):
+            nc.vector.tensor_copy(
+                out=planes[v][:].bitcast(I32)[:, (c0 - 16 * v) // 4:(c1 - 16 * v) // 4],
+                in_=planes[0][:].bitcast(I32)[:, c0 // 4:c1 // 4])
+
+        def regroup(eng, c, a, z):
+            src = raw[c][:, :, a * D:z * D].rearrange("p j w -> p w j")
+            if eng == "v":
+                nc.vector.tensor_copy(out=grp[c][:, a * D:z * D, :], in_=src)
+            else:
+                nc.scalar.copy(out=grp[c][:, a * D:z * D, :], in_=src)
+
+        def quant_w(c, a, z):
+            nc.vector.quantize_mx(out=wcod[c][:, a * D:z * D].bitcast(E4X4),
+                                  scales=wsc[c][:, a * D:z * D],
+                                  in_=grp[c][:, a * D:z * D, :].rearrange("p w j -> p (w j)"))
+
+        where = {}
+        for c, (l0, n) in enumerate(CHUNKS):
+            for i in range(n):
+                where[l0 + i] = (c, i * D)
+        done = [0, 0]
+
+        def mx(l, k):
+            c, off = where[l]
+            s0 = NS * (l + 2) + 512 * k
+            v = (l + 2) % 4
+            x0 = s0 - 16 * v
+            nc.tensor.matmul_mx(out=acc[k][:],
+                                lhsT=wcod[c][:, off:off + D].bitcast(E4X4),
+                                lhsT_scale=wsc[c][:, off:off + D],
+                                rhs=e_codes[:, s0:s0 + 512].bitcast(E5X4),
+                                rhs_scale=planes[v][:, x0:x0 + 512],
+                                start=(done[k] == 0), stop=(done[k] == NL - 1))
+            done[k] += 1
+
+        xt0 = psum.tile([P, 2, 2, P], F32, name="xt0")
+        xt1 = psum.tile([P, 2, 2, P], F32, name="xt1")
+        xt2 = psum.tile([P, 2, 2, P], F32, name="xt2")
+        xt3a = psum.tile([P, 1, 2, P], F32, name="xt3a")
+        xt3b = psum.tile([P, 1, 2, P], F32, name="xt3b")
+        transpose_g(xt0, 0, 0)
+        transpose_g(xt0, 1, 1)
+        evac_g("s", xt0, 0, 0)
+        evac_g("s", xt0, 1, 1)
+        transpose_g(xt1, 0, 2)
+        transpose_g(xt1, 1, 3)
+        evac_g("v", xt1, 0, 2)
+        evac_g("v", xt1, 1, 3)
+        transpose_g(xt2, 0, 4)
+        transpose_g(xt2, 1, 5)
+        evac_g("s", xt2, 0, 4)
+        evac_g("s", xt2, 1, 5)
+        transpose_g(xt3a, 0, 6)
+        transpose_g(xt3b, 0, 7)
+        evac_g("s", xt3a, 0, 6)
+        evac_g("v", xt3b, 0, 7)
+
+        regroup("v", 0, 0, 1)
+        regroup("s", 0, 1, 2)
+        quant_g(192, 704)
+        quant_w(0, 0, 1)
+        mx(10, 0)
+        quant_g(704, 1216)
+        mx(10, 1)
+        quant_w(0, 1, 2)
+        move(1, 192, 1216)
+        mx(11, 0)
+        nc.scalar.copy(out=e5d[:, 76:108, :, 0:7, :], in_=e5d[:, 12:44, :, 1:8, :])
+        quant_g(1216, 1728)
+        move(1, 1216, 1728)
+        mx(11, 1)
+
+        regroup("s", 1, 0, 1)
+        regroup("s", 1, 1, 2)
+        quant_w(1, 0, 1)
+        move(2, 192, 1216)
+        move(2, 1216, 1728)
+        regroup("v", 2, 0, 2)
+        regroup("s", 2, 2, 4)
+        quant_w(1, 1, 2)
+        move(3, 192, 1216)
+        move(3, 1216, 1728)
+        quant_w(2, 0, 2)
+        mx(12, 0)
+        mx(12, 1)
+        mx(13, 0)
+        mx(13, 1)
+
+        def passes(c):
+            l0, n = CHUNKS[c]
+            for i in range(n):
+                mx(l0 + i, 0)
+                mx(l0 + i, 1)
+
+        last = len(CHUNKS) - 1
+        for c in range(3, last + 1):
+            l0, n = CHUNKS[c]
+            if n >= 4:
+                regroup("v", c, 0, 2)
+                regroup("s", c, 2, 4)
+            else:
+                regroup("v", c, 0, 1)
+                regroup("s", c, 1, 2)
+            if n == 5:
+                regroup("v", c, 4, 5)
+            quant_w(c - 1, 2, 4)
+            if n >= 4:
+                quant_w(c, 0, 2)
+            else:
+                quant_w(c, 0, 1)
+            if n == 5:
+                quant_w(c, 4, 5)
+            if c - 1 <= 11:
+                passes(c - 1)
+            if c == 5:
+                nc.scalar.copy(out=e5d[:, 108:116, :, 0:7, :], in_=e5d[:, 44:52, :, 1:8, :])
+            if c == 6:
+                quant_g(1728, 1856)
+                for v in range(1, 4):
+                    move(v, 1728, 1856)
+            if c == 7:
+                nc.scalar.copy(out=e5d[:, 2:12, :, 1:8, :], in_=e5d[:, 66:76, :, 0:7, :])
+            if c == 8:
+                quant_g(0, 64)
+                quant_g(64, 192)
+                for v in range(1, 4):
+                    move(v, 16 * v, 192)
+        quant_w(last, 1, 2)
+        for l in range(4, 10):
+            mx(l, 0)
+        for l in range(4, 10):
+            mx(l, 1)
+
+        o_sb = keep.tile([P, 8, P], F32, name="o_sb")
+        res = keep.tile([P, 8, P], F32, name="res")
+        o_view = o_sb[:].rearrange("p r (s a) -> p r s a", s=NS, a=8)
+
+        def gather(k, r0, r1):
+            nc.vector.tensor_copy(
+                out=o_view[:, r0:r1, :, 4 * k:4 * k + 4],
+                in_=acc[k][:].rearrange("p (a r s) -> p r s a", a=4, r=8, s=NS)[:, r0:r1])
+
+        gather(0, 0, 8)
+        gather(1, 0, 4)
+        gather(1, 4, 8)
+        ot0 = psum.tile([P, 4, P], F32, name="ot0", tag="xt0")
+        ot1 = psum.tile([P, 4, P], F32, name="ot1", tag="xt1")
+        for r in range(4):
+            nc.tensor.transpose(ot0[:, r, :], o_sb[:, r, :], ident[:])
+        for r in range(4):
+            nc.tensor.transpose(ot1[:, r, :], o_sb[:, 4 + r, :], ident[:])
+        nc.scalar.copy(out=res[:, 0:4, :], in_=ot0[:])
+        nc.sync.dma_start(out=out_view[:, 0:4, :], in_=res[:, 0:4, :])
+        nc.vector.tensor_copy(out=res[:, 4:8, :], in_=ot1[:])
+        nc.sync.dma_start(out=out_view[:, 4:8, :], in_=res[:, 4:8, :])

@@ -48,6 +48,8 @@ def tile_ctrf_kernel(tc, x, W, b, grad_out, out):
         main = e32[:, 32 * UPAD:32 * (UPAD + 64)].rearrange(
             "p (a r s h) -> p r a s h", a=8, r=8, s=NS, h=2)
 
+        zeros = keep.tile([P, 512], BF16, name="zeros")
+        nc.vector.memset(zeros[:], 0.0)
         nc.vector.memset(planes[0][:].bitcast(I32), 0)
         nc.vector.memset(e32[:, 76 * 32:NUU * 32], 0.0)
         nc.vector.memset(e32[:, 0:UPAD * 32], 0.0)
@@ -123,25 +125,36 @@ def tile_ctrf_kernel(tc, x, W, b, grad_out, out):
                                 start=(done[k] == 0), stop=(done[k] == NL - 1))
             done[k] += 1
 
+        idle = psum.tile([P, 512], F32, name="idle")
+
+        def warm(n):
+            for i in range(n):
+                nc.tensor.matmul(out=idle[:], lhsT=zeros[:, 0:P], rhs=zeros[:], start=True, stop=True)
+
         xt0 = psum.tile([P, 2, 2, P], F32, name="xt0")
         xt1 = psum.tile([P, 2, 2, P], F32, name="xt1")
         xt2 = psum.tile([P, 2, 2, P], F32, name="xt2")
         xt3a = psum.tile([P, 1, 2, P], F32, name="xt3a")
         xt3b = psum.tile([P, 1, 2, P], F32, name="xt3b")
+        warm(5)
         transpose_g(xt0, 0, 0)
         transpose_g(xt0, 1, 1)
         evac_g("s", xt0, 0, 0)
         evac_g("s", xt0, 1, 1)
+        warm(2)
         transpose_g(xt1, 0, 2)
         transpose_g(xt1, 1, 3)
         evac_g("v", xt1, 0, 2)
         evac_g("v", xt1, 1, 3)
+        warm(2)
         transpose_g(xt2, 0, 4)
         transpose_g(xt2, 1, 5)
         evac_g("s", xt2, 0, 4)
         evac_g("s", xt2, 1, 5)
+        warm(2)
         transpose_g(xt3a, 0, 6)
         transpose_g(xt3b, 0, 7)
+        warm(4)
         evac_g("s", xt3a, 0, 6)
         evac_g("v", xt3b, 0, 7)
 

@@ -22,8 +22,10 @@ UPAD = 12
 NUU = 116
 ECOLS = NUU * NS
 
-CHUNKS = [(10, 2), (12, 2), (14, 4), (18, 4), (22, 4), (26, 4), (30, 4), (34, 4), (38, 4), (42, 4),
-          (46, 5), (0, 4), (4, 4), (8, 2)]
+CHUNKS = [(10, 1), (14, 1), (18, 1), (22, 1), (11, 3), (15, 3), (19, 3), (23, 3), (26, 4), (30, 4),
+          (34, 4), (38, 4), (42, 4), (46, 5), (0, 4), (4, 4), (8, 2)]
+V_SHARE = {1: [], 2: [(0, 1)], 3: [(0, 1)], 4: [(0, 2)], 5: [(0, 2), (4, 5)]}
+S_SHARE = {1: [(0, 1)], 2: [(1, 2)], 3: [(1, 3)], 4: [(2, 4)], 5: [(2, 4)]}
 
 
 def tile_ctrf_kernel(tc, x, W, b, grad_out, out):
@@ -48,8 +50,6 @@ def tile_ctrf_kernel(tc, x, W, b, grad_out, out):
         main = e32[:, 32 * UPAD:32 * (UPAD + 64)].rearrange(
             "p (a r s h) -> p r a s h", a=8, r=8, s=NS, h=2)
 
-        zeros = keep.tile([P, 512], BF16, name="zeros")
-        nc.vector.memset(zeros[:], 0.0)
         nc.vector.memset(planes[0][:].bitcast(I32), 0)
         nc.vector.memset(e32[:, 76 * 32:NUU * 32], 0.0)
         nc.vector.memset(e32[:, 0:UPAD * 32], 0.0)
@@ -63,8 +63,8 @@ def tile_ctrf_kernel(tc, x, W, b, grad_out, out):
         wsc = [keep.tile([P, n * D], U8, name="wsc%d" % c, align_bytes=64)
                for c, (l0, n) in enumerate(CHUNKS)]
 
-        for i in range(4):
-            nc.sync.dma_start(out=g_sb[:, 2 * i:2 * i + 2, :], in_=g_view[:, 2 * i:2 * i + 2, :])
+        for r0, r1 in [(0, 2), (2, 4), (4, 6), (6, 7), (7, 8)]:
+            nc.sync.dma_start(out=g_sb[:, r0:r1, :], in_=g_view[:, r0:r1, :])
         for c, (l0, n) in enumerate(CHUNKS):
             for h in range(2):
                 nc.sync.dma_start(out=raw[c][:, 2 * h:2 * h + 2, :],
@@ -125,69 +125,38 @@ def tile_ctrf_kernel(tc, x, W, b, grad_out, out):
                                 start=(done[k] == 0), stop=(done[k] == NL - 1))
             done[k] += 1
 
-        idle = psum.tile([P, 512], F32, name="idle")
-
-        def warm(n):
-            for i in range(n):
-                nc.tensor.matmul(out=idle[:], lhsT=zeros[:, 0:P], rhs=zeros[:], start=True, stop=True)
-
         xt0 = psum.tile([P, 2, 2, P], F32, name="xt0")
         xt1 = psum.tile([P, 2, 2, P], F32, name="xt1")
         xt2 = psum.tile([P, 2, 2, P], F32, name="xt2")
         xt3a = psum.tile([P, 1, 2, P], F32, name="xt3a")
         xt3b = psum.tile([P, 1, 2, P], F32, name="xt3b")
-        warm(5)
         transpose_g(xt0, 0, 0)
         transpose_g(xt0, 1, 1)
         evac_g("s", xt0, 0, 0)
         evac_g("s", xt0, 1, 1)
-        warm(2)
         transpose_g(xt1, 0, 2)
         transpose_g(xt1, 1, 3)
         evac_g("v", xt1, 0, 2)
         evac_g("v", xt1, 1, 3)
-        warm(2)
         transpose_g(xt2, 0, 4)
         transpose_g(xt2, 1, 5)
         evac_g("s", xt2, 0, 4)
         evac_g("s", xt2, 1, 5)
-        warm(2)
         transpose_g(xt3a, 0, 6)
         transpose_g(xt3b, 0, 7)
-        warm(4)
         evac_g("s", xt3a, 0, 6)
         evac_g("v", xt3b, 0, 7)
 
-        regroup("v", 0, 0, 1)
-        regroup("s", 0, 1, 2)
-        quant_g(192, 704)
-        quant_w(0, 0, 1)
-        mx(10, 0)
-        quant_g(704, 1216)
-        mx(10, 1)
-        quant_w(0, 1, 2)
-        move(1, 192, 1216)
-        mx(11, 0)
-        nc.scalar.copy(out=e5d[:, 76:108, :, 0:7, :], in_=e5d[:, 12:44, :, 1:8, :])
-        quant_g(1216, 1728)
-        move(1, 1216, 1728)
-        mx(11, 1)
+        def regroup_all(c):
+            n = CHUNKS[c][1]
+            for a, z in V_SHARE[n]:
+                regroup("v", c, a, z)
+            for a, z in S_SHARE[n]:
+                regroup("s", c, a, z)
 
-        regroup("s", 1, 0, 1)
-        regroup("s", 1, 1, 2)
-        quant_w(1, 0, 1)
-        move(2, 192, 1216)
-        move(2, 1216, 1728)
-        regroup("v", 2, 0, 2)
-        regroup("s", 2, 2, 4)
-        quant_w(1, 1, 2)
-        move(3, 192, 1216)
-        move(3, 1216, 1728)
-        quant_w(2, 0, 2)
-        mx(12, 0)
-        mx(12, 1)
-        mx(13, 0)
-        mx(13, 1)
+        def quant_share(c, share):
+            for a, z in share[CHUNKS[c][1]]:
+                quant_w(c, a, z)
 
         def passes(c):
             l0, n = CHUNKS[c]
@@ -195,40 +164,59 @@ def tile_ctrf_kernel(tc, x, W, b, grad_out, out):
                 mx(l0 + i, 0)
                 mx(l0 + i, 1)
 
+        for c in range(4):
+            regroup_all(c)
+        quant_g(192, 704)
+        quant_share(0, S_SHARE)
+        mx(10, 0)
+        quant_g(704, 1216)
+        mx(10, 1)
+        quant_share(1, S_SHARE)
+        mx(14, 0)
+        quant_share(2, S_SHARE)
+        mx(18, 0)
+        nc.vector.tensor_copy(out=e5d[:, 76:108, :, 0:7, :], in_=e5d[:, 12:44, :, 1:8, :])
+        quant_g(1216, 1728)
+        mx(14, 1)
+        mx(18, 1)
+        quant_share(3, S_SHARE)
+        mx(22, 0)
+        mx(22, 1)
+
+        regroup_all(4)
+        move(1, 192, 1216)
+        move(1, 1216, 1728)
+        quant_share(4, V_SHARE)
+        move(2, 192, 1216)
+        move(2, 1216, 1728)
+        regroup_all(5)
+        quant_share(4, S_SHARE)
+        move(3, 192, 1216)
+        move(3, 1216, 1728)
+        quant_share(5, V_SHARE)
+        passes(4)
+
         last = len(CHUNKS) - 1
-        for c in range(3, last + 1):
-            l0, n = CHUNKS[c]
-            if n >= 4:
-                regroup("v", c, 0, 2)
-                regroup("s", c, 2, 4)
-            else:
-                regroup("v", c, 0, 1)
-                regroup("s", c, 1, 2)
-            if n == 5:
-                regroup("v", c, 4, 5)
-            quant_w(c - 1, 2, 4)
-            if n >= 4:
-                quant_w(c, 0, 2)
-            else:
-                quant_w(c, 0, 1)
-            if n == 5:
-                quant_w(c, 4, 5)
-            if c - 1 <= 11:
+        for c in range(6, last + 1):
+            regroup_all(c)
+            quant_share(c - 1, S_SHARE)
+            quant_share(c, V_SHARE)
+            if c - 1 <= last - 2:
                 passes(c - 1)
-            if c == 5:
+            if c == 8:
                 nc.scalar.copy(out=e5d[:, 108:116, :, 0:7, :], in_=e5d[:, 44:52, :, 1:8, :])
-            if c == 6:
+            if c == 9:
                 quant_g(1728, 1856)
                 for v in range(1, 4):
                     move(v, 1728, 1856)
-            if c == 7:
+            if c == 10:
                 nc.scalar.copy(out=e5d[:, 2:12, :, 1:8, :], in_=e5d[:, 66:76, :, 0:7, :])
-            if c == 8:
+            if c == 11:
                 quant_g(0, 64)
                 quant_g(64, 192)
                 for v in range(1, 4):
                     move(v, 16 * v, 192)
-        quant_w(last, 1, 2)
+        quant_share(last, S_SHARE)
         for l in range(4, 10):
             mx(l, 0)
         for l in range(4, 10):

@@ -50,6 +50,8 @@ def tile_ctrf_kernel(tc, x, W, b, grad_out, out):
         main = e32[:, 32 * UPAD:32 * (UPAD + 64)].rearrange(
             "p (a r s h) -> p r a s h", a=8, r=8, s=NS, h=2)
 
+        zeros = keep.tile([P, 512], BF16, name="zeros")
+        nc.vector.memset(zeros[:], 0.0)
         nc.vector.memset(planes[0][:].bitcast(I32), 0)
         nc.vector.memset(e32[:, 76 * 32:NUU * 32], 0.0)
         nc.vector.memset(e32[:, 0:UPAD * 32], 0.0)
@@ -125,25 +127,36 @@ def tile_ctrf_kernel(tc, x, W, b, grad_out, out):
                                 start=(done[k] == 0), stop=(done[k] == NL - 1))
             done[k] += 1
 
+        idle = psum.tile([P, 512], F32, name="idle")
+
+        def warm(n):
+            for i in range(n):
+                nc.tensor.matmul(out=idle[:], lhsT=zeros[:, 0:P], rhs=zeros[:], start=True, stop=True)
+
         xt0 = psum.tile([P, 2, 2, P], F32, name="xt0")
         xt1 = psum.tile([P, 2, 2, P], F32, name="xt1")
         xt2 = psum.tile([P, 2, 2, P], F32, name="xt2")
         xt3a = psum.tile([P, 1, 2, P], F32, name="xt3a")
         xt3b = psum.tile([P, 1, 2, P], F32, name="xt3b")
+        warm(5)
         transpose_g(xt0, 0, 0)
         transpose_g(xt0, 1, 1)
         evac_g("s", xt0, 0, 0)
         evac_g("s", xt0, 1, 1)
+        warm(1)
         transpose_g(xt1, 0, 2)
         transpose_g(xt1, 1, 3)
         evac_g("v", xt1, 0, 2)
         evac_g("v", xt1, 1, 3)
+        warm(1)
         transpose_g(xt2, 0, 4)
         transpose_g(xt2, 1, 5)
         evac_g("s", xt2, 0, 4)
         evac_g("s", xt2, 1, 5)
+        warm(1)
         transpose_g(xt3a, 0, 6)
         transpose_g(xt3b, 0, 7)
+        warm(3)
         evac_g("s", xt3a, 0, 6)
         evac_g("v", xt3b, 0, 7)
 
@@ -175,24 +188,24 @@ def tile_ctrf_kernel(tc, x, W, b, grad_out, out):
         mx(14, 0)
         quant_share(2, S_SHARE)
         mx(18, 0)
-        nc.vector.tensor_copy(out=e5d[:, 76:108, :, 0:7, :], in_=e5d[:, 12:44, :, 1:8, :])
-        quant_g(1216, 1728)
+        nc.vector.tensor_copy(out=e5d[:, 76:92, :, 0:7, :], in_=e5d[:, 12:28, :, 1:8, :])
+        quant_g(1216, 1472)
         mx(14, 1)
         mx(18, 1)
         quant_share(3, S_SHARE)
         mx(22, 0)
         mx(22, 1)
 
-        regroup_all(4)
         move(1, 192, 1216)
-        move(1, 1216, 1728)
+        regroup_all(4)
+        move(1, 1216, 1472)
         quant_share(4, V_SHARE)
         move(2, 192, 1216)
-        move(2, 1216, 1728)
-        regroup_all(5)
+        move(2, 1216, 1472)
         quant_share(4, S_SHARE)
+        regroup_all(5)
         move(3, 192, 1216)
-        move(3, 1216, 1728)
+        move(3, 1216, 1472)
         quant_share(5, V_SHARE)
         passes(4)
 
@@ -203,12 +216,13 @@ def tile_ctrf_kernel(tc, x, W, b, grad_out, out):
             quant_share(c, V_SHARE)
             if c - 1 <= last - 2:
                 passes(c - 1)
-            if c == 8:
-                nc.scalar.copy(out=e5d[:, 108:116, :, 0:7, :], in_=e5d[:, 44:52, :, 1:8, :])
-            if c == 9:
+            if c == 6:
+                nc.scalar.copy(out=e5d[:, 92:116, :, 0:7, :], in_=e5d[:, 28:52, :, 1:8, :])
+            if c == 7:
+                quant_g(1472, 1728)
                 quant_g(1728, 1856)
                 for v in range(1, 4):
-                    move(v, 1728, 1856)
+                    move(v, 1472, 1856)
             if c == 10:
                 nc.scalar.copy(out=e5d[:, 2:12, :, 1:8, :], in_=e5d[:, 66:76, :, 0:7, :])
             if c == 11:
@@ -232,15 +246,17 @@ def tile_ctrf_kernel(tc, x, W, b, grad_out, out):
                 in_=acc[k][:].rearrange("p (a r s) -> p r s a", a=4, r=8, s=NS)[:, r0:r1])
 
         gather(0, 0, 8)
-        gather(1, 0, 4)
-        gather(1, 4, 8)
-        ot0 = psum.tile([P, 4, P], F32, name="ot0", tag="xt0")
-        ot1 = psum.tile([P, 4, P], F32, name="ot1", tag="xt1")
-        for r in range(4):
-            nc.tensor.transpose(ot0[:, r, :], o_sb[:, r, :], ident[:])
-        for r in range(4):
-            nc.tensor.transpose(ot1[:, r, :], o_sb[:, 4 + r, :], ident[:])
-        nc.scalar.copy(out=res[:, 0:4, :], in_=ot0[:])
-        nc.sync.dma_start(out=out_view[:, 0:4, :], in_=res[:, 0:4, :])
-        nc.vector.tensor_copy(out=res[:, 4:8, :], in_=ot1[:])
-        nc.sync.dma_start(out=out_view[:, 4:8, :], in_=res[:, 4:8, :])
+        for i in range(4):
+            gather(1, 2 * i, 2 * i + 2)
+        ots = [psum.tile([P, 2, P], F32, name="ot%d" % i, tag=["xt0", "xt1", "xt2", "xt3a"][i])
+               for i in range(4)]
+        for i in range(4):
+            for j in range(2):
+                nc.tensor.transpose(ots[i][:, j, :], o_sb[:, 2 * i + j, :], ident[:])
+        for i in [0, 2, 1, 3]:
+            if i % 2 == 0:
+                nc.scalar.copy(out=res[:, 2 * i:2 * i + 2, :], in_=ots[i][:])
+            else:
+                nc.vector.tensor_copy(out=res[:, 2 * i:2 * i + 2, :], in_=ots[i][:])
+        for i in range(4):
+            nc.sync.dma_start(out=out_view[:, 2 * i:2 * i + 2, :], in_=res[:, 2 * i:2 * i + 2, :])

@@ -24,8 +24,8 @@ ECOLS = NUU * NS
 
 CHUNKS = [(10, 1), (14, 1), (18, 1), (22, 1), (11, 3), (15, 3), (19, 3), (23, 3), (26, 4), (30, 4),
           (34, 4), (38, 4), (42, 4), (46, 5), (0, 4), (4, 4), (8, 2)]
-V_SHARE = {1: [], 2: [(0, 1)], 3: [(0, 1)], 4: [(0, 2)], 5: [(0, 2), (4, 5)]}
-S_SHARE = {1: [(0, 1)], 2: [(1, 2)], 3: [(1, 3)], 4: [(2, 4)], 5: [(2, 4)]}
+V_SHARE = {1: [], 2: [(0, 1)], 4: [(0, 2)], 5: [(0, 2), (4, 5)]}
+S_SHARE = {1: [(0, 1)], 2: [(1, 2)], 4: [(2, 4)], 5: [(2, 4)]}
 
 
 def tile_ctrf_kernel(tc, x, W, b, grad_out, out):
@@ -50,8 +50,6 @@ def tile_ctrf_kernel(tc, x, W, b, grad_out, out):
         main = e32[:, 32 * UPAD:32 * (UPAD + 64)].rearrange(
             "p (a r s h) -> p r a s h", a=8, r=8, s=NS, h=2)
 
-        zeros = keep.tile([P, 512], BF16, name="zeros")
-        nc.vector.memset(zeros[:], 0.0)
         nc.vector.memset(planes[0][:].bitcast(I32), 0)
         nc.vector.memset(e32[:, 76 * 32:NUU * 32], 0.0)
         nc.vector.memset(e32[:, 0:UPAD * 32], 0.0)
@@ -127,36 +125,25 @@ def tile_ctrf_kernel(tc, x, W, b, grad_out, out):
                                 start=(done[k] == 0), stop=(done[k] == NL - 1))
             done[k] += 1
 
-        idle = psum.tile([P, 512], F32, name="idle")
-
-        def warm(n):
-            for i in range(n):
-                nc.tensor.matmul(out=idle[:], lhsT=zeros[:, 0:P], rhs=zeros[:], start=True, stop=True)
-
         xt0 = psum.tile([P, 2, 2, P], F32, name="xt0")
         xt1 = psum.tile([P, 2, 2, P], F32, name="xt1")
         xt2 = psum.tile([P, 2, 2, P], F32, name="xt2")
         xt3a = psum.tile([P, 1, 2, P], F32, name="xt3a")
         xt3b = psum.tile([P, 1, 2, P], F32, name="xt3b")
-        warm(5)
         transpose_g(xt0, 0, 0)
         transpose_g(xt0, 1, 1)
         evac_g("s", xt0, 0, 0)
         evac_g("s", xt0, 1, 1)
-        warm(1)
         transpose_g(xt1, 0, 2)
         transpose_g(xt1, 1, 3)
         evac_g("v", xt1, 0, 2)
         evac_g("v", xt1, 1, 3)
-        warm(1)
         transpose_g(xt2, 0, 4)
         transpose_g(xt2, 1, 5)
         evac_g("s", xt2, 0, 4)
         evac_g("s", xt2, 1, 5)
-        warm(1)
         transpose_g(xt3a, 0, 6)
         transpose_g(xt3b, 0, 7)
-        warm(3)
         evac_g("s", xt3a, 0, 6)
         evac_g("v", xt3b, 0, 7)
 
@@ -177,8 +164,11 @@ def tile_ctrf_kernel(tc, x, W, b, grad_out, out):
                 mx(l0 + i, 0)
                 mx(l0 + i, 1)
 
-        for c in range(4):
-            regroup_all(c)
+        regroup_all(0)
+        regroup_all(1)
+        nc.scalar.copy(out=e5d[:, 76:92, :, 0:7, :], in_=e5d[:, 12:28, :, 1:8, :])
+        regroup_all(2)
+        regroup_all(3)
         quant_g(192, 704)
         quant_share(0, S_SHARE)
         mx(10, 0)
@@ -186,36 +176,28 @@ def tile_ctrf_kernel(tc, x, W, b, grad_out, out):
         mx(10, 1)
         quant_share(1, S_SHARE)
         mx(14, 0)
-        quant_share(2, S_SHARE)
-        mx(18, 0)
-        nc.vector.tensor_copy(out=e5d[:, 76:92, :, 0:7, :], in_=e5d[:, 12:28, :, 1:8, :])
         quant_g(1216, 1472)
         mx(14, 1)
+        quant_share(2, S_SHARE)
+        mx(18, 0)
         mx(18, 1)
+        move(1, 192, 1472)
         quant_share(3, S_SHARE)
         mx(22, 0)
         mx(22, 1)
 
-        move(1, 192, 1216)
-        regroup_all(4)
-        move(1, 1216, 1472)
-        quant_share(4, V_SHARE)
-        move(2, 192, 1216)
-        move(2, 1216, 1472)
-        quant_share(4, S_SHARE)
-        regroup_all(5)
-        move(3, 192, 1216)
-        move(3, 1216, 1472)
-        quant_share(5, V_SHARE)
-        passes(4)
-
-        last = len(CHUNKS) - 1
-        for c in range(6, last + 1):
-            regroup_all(c)
-            quant_share(c - 1, S_SHARE)
-            quant_share(c, V_SHARE)
-            if c - 1 <= last - 2:
-                passes(c - 1)
+        for c in range(4, 8):
+            regroup("s", c, 0, 1)
+            regroup("s", c, 1, 2)
+            regroup("v", c, 2, 3)
+            quant_w(c, 0, 1)
+            if c == 4:
+                move(2, 192, 1472)
+            quant_w(c, 1, 2)
+            if c == 4:
+                move(3, 192, 1472)
+            quant_w(c, 2, 3)
+            passes(c)
             if c == 6:
                 nc.scalar.copy(out=e5d[:, 92:116, :, 0:7, :], in_=e5d[:, 28:52, :, 1:8, :])
             if c == 7:
@@ -223,6 +205,16 @@ def tile_ctrf_kernel(tc, x, W, b, grad_out, out):
                 quant_g(1728, 1856)
                 for v in range(1, 4):
                     move(v, 1472, 1856)
+
+        last = len(CHUNKS) - 1
+        regroup_all(8)
+        quant_share(8, V_SHARE)
+        for c in range(9, last + 1):
+            regroup_all(c)
+            quant_share(c - 1, S_SHARE)
+            quant_share(c, V_SHARE)
+            if c - 1 <= last - 2:
+                passes(c - 1)
             if c == 10:
                 nc.scalar.copy(out=e5d[:, 2:12, :, 1:8, :], in_=e5d[:, 66:76, :, 0:7, :])
             if c == 11:

@@ -50,6 +50,8 @@ def tile_ctrf_kernel(tc, x, W, b, grad_out, out):
         main = e32[:, 32 * UPAD:32 * (UPAD + 64)].rearrange(
             "p (a r s h) -> p r a s h", a=8, r=8, s=NS, h=2)
 
+        zeros = keep.tile([P, 512], BF16, name="zeros")
+        nc.vector.memset(zeros[:], 0.0)
         nc.vector.memset(planes[0][:].bitcast(I32), 0)
         nc.vector.memset(e32[:, 76 * 32:NUU * 32], 0.0)
         nc.vector.memset(e32[:, 0:UPAD * 32], 0.0)
@@ -125,25 +127,36 @@ def tile_ctrf_kernel(tc, x, W, b, grad_out, out):
                                 start=(done[k] == 0), stop=(done[k] == NL - 1))
             done[k] += 1
 
+        idle = psum.tile([P, 512], F32, name="idle")
+
+        def warm(n):
+            for i in range(n):
+                nc.tensor.matmul(out=idle[:], lhsT=zeros[:, 0:P], rhs=zeros[:], start=True, stop=True)
+
         xt0 = psum.tile([P, 2, 2, P], F32, name="xt0")
         xt1 = psum.tile([P, 2, 2, P], F32, name="xt1")
         xt2 = psum.tile([P, 2, 2, P], F32, name="xt2")
         xt3a = psum.tile([P, 1, 2, P], F32, name="xt3a")
         xt3b = psum.tile([P, 1, 2, P], F32, name="xt3b")
+        warm(12)
         transpose_g(xt0, 0, 0)
         transpose_g(xt0, 1, 1)
         evac_g("s", xt0, 0, 0)
         evac_g("s", xt0, 1, 1)
+        warm(1)
         transpose_g(xt1, 0, 2)
         transpose_g(xt1, 1, 3)
         evac_g("v", xt1, 0, 2)
         evac_g("v", xt1, 1, 3)
+        warm(1)
         transpose_g(xt2, 0, 4)
         transpose_g(xt2, 1, 5)
         evac_g("s", xt2, 0, 4)
         evac_g("s", xt2, 1, 5)
+        warm(1)
         transpose_g(xt3a, 0, 6)
         transpose_g(xt3b, 0, 7)
+        warm(4)
         evac_g("s", xt3a, 0, 6)
         evac_g("v", xt3b, 0, 7)
 

@@ -138,7 +138,7 @@ def tile_ctrf_kernel(tc, x, W, b, grad_out, out):
         xt2 = psum.tile([P, 2, 2, P], F32, name="xt2")
         xt3a = psum.tile([P, 1, 2, P], F32, name="xt3a")
         xt3b = psum.tile([P, 1, 2, P], F32, name="xt3b")
-        warm(12)
+        warm(5)
         transpose_g(xt0, 0, 0)
         transpose_g(xt0, 1, 1)
         evac_g("s", xt0, 0, 0)
@@ -156,7 +156,7 @@ def tile_ctrf_kernel(tc, x, W, b, grad_out, out):
         warm(1)
         transpose_g(xt3a, 0, 6)
         transpose_g(xt3b, 0, 7)
-        warm(4)
+        warm(3)
         evac_g("s", xt3a, 0, 6)
         evac_g("v", xt3b, 0, 7)
 

@@ -14,18 +14,26 @@ E5X4 = mybir.dt.float8_e5m2_x4
 P = 128
 NL = 51
 D = 128
+N = 512
 FLOPS = 2 * 1024 * 512 * NL * D
 BYTES = 512 * NL * D * 2 + 1024 * 512 * 2 + 1024 * D * 4
 
 NS = 16
-UPAD = 12
-NUU = 116
-ECOLS = NUU * NS
+G_OWN = 12
+G_MID = G_OWN + 32
+G_RIGHT = G_OWN + 64
+G_RIGHT2 = G_RIGHT + 16
+G_ALL = G_RIGHT + 40
 
 CHUNKS = [(10, 1), (14, 1), (18, 1), (22, 1), (11, 3), (15, 3), (19, 3), (23, 3), (26, 4), (30, 4),
           (34, 4), (38, 4), (42, 4), (46, 5), (0, 4), (4, 4), (8, 2)]
-V_SHARE = {1: [], 2: [(0, 1)], 4: [(0, 2)], 5: [(0, 2), (4, 5)]}
-S_SHARE = {1: [(0, 1)], 2: [(1, 2)], 4: [(2, 4)], 5: [(2, 4)]}
+SHARES = {1: [("s", 0, 1)],
+          2: [("v", 0, 1), ("s", 1, 2)],
+          3: [("v", 0, 1), ("s", 1, 3)],
+          4: [("v", 0, 2), ("s", 2, 4)],
+          5: [("v", 0, 2), ("v", 4, 5), ("s", 2, 4)]}
+XT_BANKS = [("xt0", [0, 1], "s"), ("xt1", [2, 3], "v"), ("xt2", [4, 5], "s"), ("xt3a", [6], "s"),
+            ("xt3b", [7], "v")]
 
 
 def tile_ctrf_kernel(tc, x, W, b, grad_out, out):
@@ -39,22 +47,25 @@ def tile_ctrf_kernel(tc, x, W, b, grad_out, out):
         out_view = out.flatten_outer_dims().rearrange("(p r) d -> p r d", r=8)
         w_view = W.rearrange("(h q e) c -> h q e c", h=2, q=P, e=2)
 
+        def copy(eng, dst, src):
+            if eng == "v":
+                nc.vector.tensor_copy(out=dst, in_=src)
+            else:
+                nc.scalar.copy(out=dst, in_=src)
+
         ident = keep.tile([P, P], F32, name="ident")
         make_identity(nc, ident[:])
 
-        e_bf = keep.tile([P, ECOLS * 4], BF16, name="e_bf", align_bytes=64)
-        e_codes = keep.tile([P, ECOLS], U32, name="e_codes", align_bytes=64)
-        planes = [keep.tile([P, ECOLS], U8, name="plane%d" % v, align_bytes=64) for v in range(4)]
+        e_bf = keep.tile([P, G_ALL * NS * 4], BF16, name="e_bf", align_bytes=64)
+        e_codes = keep.tile([P, G_ALL * NS], U32, name="e_codes", align_bytes=64)
+        planes = [keep.tile([P, G_ALL * NS], U8, name="plane%d" % v, align_bytes=64) for v in range(4)]
         e32 = e_bf[:].bitcast(F32)
-        e5d = e32.rearrange("p (uu g s h) -> p uu g s h", uu=NUU, g=2, s=8, h=2)
-        main = e32[:, 32 * UPAD:32 * (UPAD + 64)].rearrange(
-            "p (a r s h) -> p r a s h", a=8, r=8, s=NS, h=2)
+        e_streams = e32.rearrange("p (g n s h) -> p g n s h", g=G_ALL, n=2, s=8, h=2)
+        e_own = e32[:, 32 * G_OWN:32 * G_RIGHT].rearrange("p (a r s h) -> p r a s h", a=8, r=8, s=NS, h=2)
 
-        zeros = keep.tile([P, 512], BF16, name="zeros")
-        nc.vector.memset(zeros[:], 0.0)
         nc.vector.memset(planes[0][:].bitcast(I32), 0)
-        nc.vector.memset(e32[:, 76 * 32:NUU * 32], 0.0)
-        nc.vector.memset(e32[:, 0:UPAD * 32], 0.0)
+        nc.vector.memset(e32[:, 32 * G_RIGHT:32 * G_ALL], 0.0)
+        nc.vector.memset(e32[:, 0:32 * G_OWN], 0.0)
 
         g_sb = keep.tile([P, 8, 512], BF16, name="g_sb")
         raw = [keep.tile([P, 4, n * D], BF16, name="raw%d" % c) for c, (l0, n) in enumerate(CHUNKS)]
@@ -72,7 +83,7 @@ def tile_ctrf_kernel(tc, x, W, b, grad_out, out):
                 nc.sync.dma_start(out=raw[c][:, 2 * h:2 * h + 2, :],
                                   in_=w_view[h][:, :, l0 * D:(l0 + n) * D])
 
-        acc = [psum.tile([P, 512], F32, name="acc%d" % k) for k in range(2)]
+        acc = [psum.tile([P, N], F32, name="acc%d" % k) for k in range(2)]
         g32 = g_sb[:].rearrange("p r o -> p (r o)").bitcast(F32)
 
         def transpose_g(xt, j, r):
@@ -80,33 +91,33 @@ def tile_ctrf_kernel(tc, x, W, b, grad_out, out):
                 nc.tensor.transpose(xt[:, j, h, :], g32[:, r * 256 + h * P:r * 256 + (h + 1) * P],
                                     ident[:])
 
-        def evac_g(eng, xt, j, r):
-            src = xt[:, j].rearrange("p h (s a) -> p a s h", s=NS, a=8)
-            if eng == "v":
-                nc.vector.tensor_copy(out=main[:, r], in_=src)
-            else:
-                nc.scalar.copy(out=main[:, r], in_=src)
+        def lay_out_g(eng, xt, j, r):
+            copy(eng, e_own[:, r], xt[:, j].rearrange("p h (s a) -> p a s h", s=NS, a=8))
 
-        def quant_g(c0, c1):
-            nc.vector.quantize_mx(out=e_codes[:, c0:c1].bitcast(E5X4), scales=planes[0][:, c0:c1],
-                                  in_=e_bf[:, 4 * c0:4 * c1])
+        def copy_halo(eng, g0, g1, shift):
+            lo = max(0, -shift)
+            copy(eng, e_streams[:, g0:g1, :, lo:lo + 7, :],
+                 e_streams[:, g0 - 64 * shift:g1 - 64 * shift, :, lo + shift:lo + shift + 7, :])
 
-        def move(v, c0, c1):
-            nc.vector.tensor_copy(
-                out=planes[v][:].bitcast(I32)[:, (c0 - 16 * v) // 4:(c1 - 16 * v) // 4],
-                in_=planes[0][:].bitcast(I32)[:, c0 // 4:c1 // 4])
+        def quantise_g(g0, g1):
+            nc.vector.quantize_mx(out=e_codes[:, NS * g0:NS * g1].bitcast(E5X4),
+                                  scales=planes[0][:, NS * g0:NS * g1],
+                                  in_=e_bf[:, 4 * NS * g0:4 * NS * g1])
 
-        def regroup(eng, c, a, z):
-            src = raw[c][:, :, a * D:z * D].rearrange("p j w -> p w j")
-            if eng == "v":
-                nc.vector.tensor_copy(out=grp[c][:, a * D:z * D, :], in_=src)
-            else:
-                nc.scalar.copy(out=grp[c][:, a * D:z * D, :], in_=src)
+        def move_plane(v, g0, g1):
+            nc.vector.tensor_copy(out=planes[v][:].bitcast(I32)[:, 4 * (g0 - v):4 * (g1 - v)],
+                                  in_=planes[0][:].bitcast(I32)[:, 4 * g0:4 * g1])
 
-        def quant_w(c, a, z):
-            nc.vector.quantize_mx(out=wcod[c][:, a * D:z * D].bitcast(E4X4),
-                                  scales=wsc[c][:, a * D:z * D],
-                                  in_=grp[c][:, a * D:z * D, :].rearrange("p w j -> p (w j)"))
+        def regroup(c):
+            for eng, a, z in SHARES[CHUNKS[c][1]]:
+                copy(eng, grp[c][:, a * D:z * D, :], raw[c][:, :, a * D:z * D].rearrange("p j w -> p w j"))
+
+        def quantise_w(c, who):
+            for eng, a, z in SHARES[CHUNKS[c][1]]:
+                if eng == who:
+                    nc.vector.quantize_mx(out=wcod[c][:, a * D:z * D].bitcast(E4X4),
+                                          scales=wsc[c][:, a * D:z * D],
+                                          in_=grp[c][:, a * D:z * D, :].rearrange("p w j -> p (w j)"))
 
         where = {}
         for c, (l0, n) in enumerate(CHUNKS):
@@ -116,60 +127,15 @@ def tile_ctrf_kernel(tc, x, W, b, grad_out, out):
 
         def mx(l, k):
             c, off = where[l]
-            s0 = NS * (l + 2) + 512 * k
-            v = (l + 2) % 4
-            x0 = s0 - 16 * v
+            g0 = l + 2 + 32 * k
+            v = g0 % 4
             nc.tensor.matmul_mx(out=acc[k][:],
                                 lhsT=wcod[c][:, off:off + D].bitcast(E4X4),
                                 lhsT_scale=wsc[c][:, off:off + D],
-                                rhs=e_codes[:, s0:s0 + 512].bitcast(E5X4),
-                                rhs_scale=planes[v][:, x0:x0 + 512],
+                                rhs=e_codes[:, NS * g0:NS * g0 + N].bitcast(E5X4),
+                                rhs_scale=planes[v][:, NS * (g0 - v):NS * (g0 - v) + N],
                                 start=(done[k] == 0), stop=(done[k] == NL - 1))
             done[k] += 1
-
-        idle = psum.tile([P, 512], F32, name="idle")
-
-        def warm(n):
-            for i in range(n):
-                nc.tensor.matmul(out=idle[:], lhsT=zeros[:, 0:P], rhs=zeros[:], start=True, stop=True)
-
-        xt0 = psum.tile([P, 2, 2, P], F32, name="xt0")
-        xt1 = psum.tile([P, 2, 2, P], F32, name="xt1")
-        xt2 = psum.tile([P, 2, 2, P], F32, name="xt2")
-        xt3a = psum.tile([P, 1, 2, P], F32, name="xt3a")
-        xt3b = psum.tile([P, 1, 2, P], F32, name="xt3b")
-        warm(5)
-        transpose_g(xt0, 0, 0)
-        transpose_g(xt0, 1, 1)
-        evac_g("s", xt0, 0, 0)
-        evac_g("s", xt0, 1, 1)
-        warm(1)
-        transpose_g(xt1, 0, 2)
-        transpose_g(xt1, 1, 3)
-        evac_g("v", xt1, 0, 2)
-        evac_g("v", xt1, 1, 3)
-        warm(1)
-        transpose_g(xt2, 0, 4)
-        transpose_g(xt2, 1, 5)
-        evac_g("s", xt2, 0, 4)
-        evac_g("s", xt2, 1, 5)
-        warm(1)
-        transpose_g(xt3a, 0, 6)
-        transpose_g(xt3b, 0, 7)
-        warm(3)
-        evac_g("s", xt3a, 0, 6)
-        evac_g("v", xt3b, 0, 7)
-
-        def regroup_all(c):
-            n = CHUNKS[c][1]
-            for a, z in V_SHARE[n]:
-                regroup("v", c, a, z)
-            for a, z in S_SHARE[n]:
-                regroup("s", c, a, z)
-
-        def quant_share(c, share):
-            for a, z in share[CHUNKS[c][1]]:
-                quant_w(c, a, z)
 
         def passes(c):
             l0, n = CHUNKS[c]
@@ -177,65 +143,72 @@ def tile_ctrf_kernel(tc, x, W, b, grad_out, out):
                 mx(l0 + i, 0)
                 mx(l0 + i, 1)
 
-        regroup_all(0)
-        regroup_all(1)
-        nc.scalar.copy(out=e5d[:, 76:92, :, 0:7, :], in_=e5d[:, 12:28, :, 1:8, :])
-        regroup_all(2)
-        regroup_all(3)
-        quant_g(192, 704)
-        quant_share(0, S_SHARE)
+        xts = [psum.tile([P, len(rows), 2, P], F32, name=name) for name, rows, eng in XT_BANKS]
+        for i in range(3):
+            name, rows, eng = XT_BANKS[i]
+            for j, r in enumerate(rows):
+                transpose_g(xts[i], j, r)
+            for j, r in enumerate(rows):
+                lay_out_g(eng, xts[i], j, r)
+        for i in range(3, 5):
+            transpose_g(xts[i], 0, XT_BANKS[i][1][0])
+        for i in range(3, 5):
+            lay_out_g(XT_BANKS[i][2], xts[i], 0, XT_BANKS[i][1][0])
+
+        for c in range(4):
+            regroup(c)
+        quantise_g(G_OWN, G_MID)
+        quantise_w(0, "s")
         mx(10, 0)
-        quant_g(704, 1216)
+        quantise_g(G_MID, G_RIGHT)
         mx(10, 1)
-        quant_share(1, S_SHARE)
+        quantise_w(1, "s")
         mx(14, 0)
-        quant_g(1216, 1472)
-        mx(14, 1)
-        quant_share(2, S_SHARE)
+        quantise_w(2, "s")
         mx(18, 0)
+        copy_halo("v", G_RIGHT, G_RIGHT2, 1)
+        quantise_g(G_RIGHT, G_RIGHT2)
+        mx(14, 1)
         mx(18, 1)
-        move(1, 192, 1472)
-        quant_share(3, S_SHARE)
+        quantise_w(3, "s")
         mx(22, 0)
         mx(22, 1)
 
-        for c in range(4, 8):
-            regroup("s", c, 0, 1)
-            regroup("s", c, 1, 2)
-            regroup("v", c, 2, 3)
-            quant_w(c, 0, 1)
-            if c == 4:
-                move(2, 192, 1472)
-            quant_w(c, 1, 2)
-            if c == 4:
-                move(3, 192, 1472)
-            quant_w(c, 2, 3)
-            passes(c)
-            if c == 6:
-                nc.scalar.copy(out=e5d[:, 92:116, :, 0:7, :], in_=e5d[:, 28:52, :, 1:8, :])
-            if c == 7:
-                quant_g(1472, 1728)
-                quant_g(1728, 1856)
-                for v in range(1, 4):
-                    move(v, 1472, 1856)
+        move_plane(1, G_OWN, G_RIGHT)
+        regroup(4)
+        move_plane(1, G_RIGHT, G_RIGHT2)
+        quantise_w(4, "v")
+        move_plane(2, G_OWN, G_RIGHT)
+        move_plane(2, G_RIGHT, G_RIGHT2)
+        quantise_w(4, "s")
+        regroup(5)
+        move_plane(3, G_OWN, G_RIGHT)
+        move_plane(3, G_RIGHT, G_RIGHT2)
+        quantise_w(5, "v")
+        passes(4)
 
         last = len(CHUNKS) - 1
-        regroup_all(8)
-        quant_share(8, V_SHARE)
-        for c in range(9, last + 1):
-            regroup_all(c)
-            quant_share(c - 1, S_SHARE)
-            quant_share(c, V_SHARE)
+        for c in range(6, last + 1):
+            regroup(c)
+            quantise_w(c - 1, "s")
+            quantise_w(c, "v")
             if c - 1 <= last - 2:
                 passes(c - 1)
-            if c == 10:
-                nc.scalar.copy(out=e5d[:, 2:12, :, 1:8, :], in_=e5d[:, 66:76, :, 0:7, :])
-            if c == 11:
-                quant_g(0, 64)
-                quant_g(64, 192)
+            if c == 6:
+                copy_halo("s", G_RIGHT2, G_ALL, 1)
+            if c == 7:
+                quantise_g(G_RIGHT2, G_RIGHT2 + 16)
+                quantise_g(G_RIGHT2 + 16, G_ALL)
                 for v in range(1, 4):
-                    move(v, 16 * v, 192)
-        quant_share(last, S_SHARE)
+                    move_plane(v, G_RIGHT2, G_ALL)
+            if c == 10:
+                copy_halo("s", 2, G_OWN, -1)
+            if c == 11:
+                quantise_g(0, 4)
+                quantise_g(4, G_OWN)
+                for v in range(1, 4):
+                    move_plane(v, v, G_OWN)
+        quantise_w(last, "s")
         for l in range(4, 10):
             mx(l, 0)
         for l in range(4, 10):
@@ -253,15 +226,12 @@ def tile_ctrf_kernel(tc, x, W, b, grad_out, out):
         gather(0, 0, 8)
         for i in range(4):
             gather(1, 2 * i, 2 * i + 2)
-        ots = [psum.tile([P, 2, P], F32, name="ot%d" % i, tag=["xt0", "xt1", "xt2", "xt3a"][i])
-               for i in range(4)]
+        ots = [psum.tile([P, 2, P], F32, name="ot%d" % i, tag=XT_BANKS[i][0]) for i in range(4)]
         for i in range(4):
             for j in range(2):
                 nc.tensor.transpose(ots[i][:, j, :], o_sb[:, 2 * i + j, :], ident[:])
-        for i in [0, 2, 1, 3]:
-            if i % 2 == 0:
-                nc.scalar.copy(out=res[:, 2 * i:2 * i + 2, :], in_=ots[i][:])
-            else:
-                nc.vector.tensor_copy(out=res[:, 2 * i:2 * i + 2, :], in_=ots[i][:])
+        for eng, pieces in [("s", [0, 2]), ("v", [1, 3])]:
+            for i in pieces:
+                copy(eng, res[:, 2 * i:2 * i + 2, :], ots[i][:])
         for i in range(4):
             nc.sync.dma_start(out=out_view[:, 2 * i:2 * i + 2, :], in_=res[:, 2 * i:2 * i + 2, :])

from contextlib import ExitStack

import concourse.mybir as mybir
from concourse.masks import make_identity

BF16 = mybir.dt.bfloat16
F32 = mybir.dt.float32
I32 = mybir.dt.int32
U32 = mybir.dt.uint32
U8 = mybir.dt.uint8
E4X4 = mybir.dt.float8_e4m3fn_x4
E5X4 = mybir.dt.float8_e5m2_x4

P = 128
NL = 51
D = 128
N = 512
FLOPS = 2 * 1024 * 512 * NL * D
BYTES = 512 * NL * D * 2 + 1024 * 512 * 2 + 1024 * D * 4

NS = 16
G_OWN = 12
G_MID = G_OWN + 32
G_RIGHT = G_OWN + 64
G_RIGHT2 = G_RIGHT + 16
G_ALL = G_RIGHT + 40

CHUNKS = [(10, 1), (14, 1), (18, 1), (22, 1), (11, 3), (15, 3), (19, 3), (23, 3), (26, 4), (30, 4),
          (34, 4), (38, 4), (42, 4), (46, 5), (0, 4), (4, 4), (8, 2)]
SHARES = {1: [("s", 0, 1)],
          2: [("v", 0, 1), ("s", 1, 2)],
          3: [("v", 0, 1), ("s", 1, 3)],
          4: [("v", 0, 2), ("s", 2, 4)],
          5: [("v", 0, 2), ("v", 4, 5), ("s", 2, 4)]}
XT_BANKS = [("xt0", [0, 1], "s"), ("xt1", [2, 3], "v"), ("xt2", [4, 5], "s"), ("xt3a", [6], "s"),
            ("xt3b", [7], "v")]


def tile_ctrf_kernel(tc, x, W, b, grad_out, out):
    nc = tc.nc
    with ExitStack() as ctx:
        keep = ctx.enter_context(tc.tile_pool(name="keep", bufs=1))
        psum = ctx.enter_context(tc.psum_pool(name="psum", bufs=1))
        ctx.enter_context(tc.manual_schedule())

        g_view = grad_out.flatten_outer_dims().rearrange("(p r) o -> p r o", r=8)
        out_view = out.flatten_outer_dims().rearrange("(p r) d -> p r d", r=8)
        w_view = W.rearrange("(h q e) c -> h q e c", h=2, q=P, e=2)

        def copy(eng, dst, src):
            if eng == "v":
                nc.vector.tensor_copy(out=dst, in_=src)
            else:
                nc.scalar.copy(out=dst, in_=src)

        ident = keep.tile([P, P], F32, name="ident")
        make_identity(nc, ident[:])

        e_bf = keep.tile([P, G_ALL * NS * 4], BF16, name="e_bf", align_bytes=64)
        e_codes = keep.tile([P, G_ALL * NS], U32, name="e_codes", align_bytes=64)
        planes = [keep.tile([P, G_ALL * NS], U8, name="plane%d" % v, align_bytes=64) for v in range(4)]
        e32 = e_bf[:].bitcast(F32)
        e_streams = e32.rearrange("p (g n s h) -> p g n s h", g=G_ALL, n=2, s=8, h=2)
        e_own = e32[:, 32 * G_OWN:32 * G_RIGHT].rearrange("p (a r s h) -> p r a s h", a=8, r=8, s=NS, h=2)

        nc.vector.memset(planes[0][:].bitcast(I32), 0)
        nc.vector.memset(e32[:, 32 * G_RIGHT:32 * G_ALL], 0.0)
        nc.vector.memset(e32[:, 0:32 * G_OWN], 0.0)

        g_sb = keep.tile([P, 8, 512], BF16, name="g_sb")
        raw = [keep.tile([P, 4, n * D], BF16, name="raw%d" % c) for c, (l0, n) in enumerate(CHUNKS)]
        grp = [keep.tile([P, n * D, 4], BF16, name="grp%d" % c, align_bytes=64)
               for c, (l0, n) in enumerate(CHUNKS)]
        wcod = [keep.tile([P, n * D], U32, name="wcod%d" % c, align_bytes=64)
                for c, (l0, n) in enumerate(CHUNKS)]
        wsc = [keep.tile([P, n * D], U8, name="wsc%d" % c, align_bytes=64)
               for c, (l0, n) in enumerate(CHUNKS)]

        for r0, r1 in [(0, 2), (2, 4), (4, 6), (6, 7), (7, 8)]:
            nc.sync.dma_start(out=g_sb[:, r0:r1, :], in_=g_view[:, r0:r1, :])
        for c, (l0, n) in enumerate(CHUNKS):
            for h in range(2):
                nc.sync.dma_start(out=raw[c][:, 2 * h:2 * h + 2, :],
                                  in_=w_view[h][:, :, l0 * D:(l0 + n) * D])

        acc = [psum.tile([P, N], F32, name="acc%d" % k) for k in range(2)]
        g32 = g_sb[:].rearrange("p r o -> p (r o)").bitcast(F32)

        def transpose_g(xt, j, r):
            for h in range(2):
                nc.tensor.transpose(xt[:, j, h, :], g32[:, r * 256 + h * P:r * 256 + (h + 1) * P],
                                    ident[:])

        def lay_out_g(eng, xt, j, r):
            copy(eng, e_own[:, r], xt[:, j].rearrange("p h (s a) -> p a s h", s=NS, a=8))

        def copy_halo(eng, g0, g1, shift):
            lo = max(0, -shift)
            copy(eng, e_streams[:, g0:g1, :, lo:lo + 7, :],
                 e_streams[:, g0 - 64 * shift:g1 - 64 * shift, :, lo + shift:lo + shift + 7, :])

        def quantise_g(g0, g1):
            nc.vector.quantize_mx(out=e_codes[:, NS * g0:NS * g1].bitcast(E5X4),
                                  scales=planes[0][:, NS * g0:NS * g1],
                                  in_=e_bf[:, 4 * NS * g0:4 * NS * g1])

        def move_plane(v, g0, g1):
            nc.vector.tensor_copy(out=planes[v][:].bitcast(I32)[:, 4 * (g0 - v):4 * (g1 - v)],
                                  in_=planes[0][:].bitcast(I32)[:, 4 * g0:4 * g1])

        def regroup(c):
            for eng, a, z in SHARES[CHUNKS[c][1]]:
                copy(eng, grp[c][:, a * D:z * D, :], raw[c][:, :, a * D:z * D].rearrange("p j w -> p w j"))

        def quantise_w(c, who):
            for eng, a, z in SHARES[CHUNKS[c][1]]:
                if eng == who:
                    nc.vector.quantize_mx(out=wcod[c][:, a * D:z * D].bitcast(E4X4),
                                          scales=wsc[c][:, a * D:z * D],
                                          in_=grp[c][:, a * D:z * D, :].rearrange("p w j -> p (w j)"))

        where = {}
        for c, (l0, n) in enumerate(CHUNKS):
            for i in range(n):
                where[l0 + i] = (c, i * D)
        done = [0, 0]

        def mx(l, k):
            c, off = where[l]
            g0 = l + 2 + 32 * k
            v = g0 % 4
            nc.tensor.matmul_mx(out=acc[k][:],
                                lhsT=wcod[c][:, off:off + D].bitcast(E4X4),
                                lhsT_scale=wsc[c][:, off:off + D],
                                rhs=e_codes[:, NS * g0:NS * g0 + N].bitcast(E5X4),
                                rhs_scale=planes[v][:, NS * (g0 - v):NS * (g0 - v) + N],
                                start=(done[k] == 0), stop=(done[k] == NL - 1))
            done[k] += 1

        def passes(c):
            l0, n = CHUNKS[c]
            for i in range(n):
                mx(l0 + i, 0)
                mx(l0 + i, 1)

        xts = [psum.tile([P, len(rows), 2, P], F32, name=name) for name, rows, eng in XT_BANKS]
        for i in range(3):
            name, rows, eng = XT_BANKS[i]
            for j, r in enumerate(rows):
                transpose_g(xts[i], j, r)
            for j, r in enumerate(rows):
                lay_out_g(eng, xts[i], j, r)
        for i in range(3, 5):
            transpose_g(xts[i], 0, XT_BANKS[i][1][0])
        for i in range(3, 5):
            lay_out_g(XT_BANKS[i][2], xts[i], 0, XT_BANKS[i][1][0])

        for c in range(4):
            regroup(c)
        quantise_g(G_OWN, G_MID)
        quantise_w(0, "s")
        mx(10, 0)
        quantise_g(G_MID, G_RIGHT)
        mx(10, 1)
        quantise_w(1, "s")
        mx(14, 0)
        quantise_w(2, "s")
        mx(18, 0)
        copy_halo("v", G_RIGHT, G_RIGHT2, 1)
        quantise_g(G_RIGHT, G_RIGHT2)
        mx(14, 1)
        mx(18, 1)
        quantise_w(3, "s")
        mx(22, 0)
        mx(22, 1)

        move_plane(1, G_OWN, G_RIGHT)
        regroup(4)
        move_plane(1, G_RIGHT, G_RIGHT2)
        quantise_w(4, "v")
        move_plane(2, G_OWN, G_RIGHT)
        move_plane(2, G_RIGHT, G_RIGHT2)
        quantise_w(4, "s")
        regroup(5)
        move_plane(3, G_OWN, G_RIGHT)
        move_plane(3, G_RIGHT, G_RIGHT2)
        quantise_w(5, "v")
        passes(4)

        last = len(CHUNKS) - 1
        for c in range(6, last + 1):
            regroup(c)
            quantise_w(c - 1, "s")
            quantise_w(c, "v")
            if c - 1 <= last - 2:
                passes(c - 1)
            if c == 6:
                copy_halo("s", G_RIGHT2, G_ALL, 1)
            if c == 7:
                quantise_g(G_RIGHT2, G_RIGHT2 + 16)
                quantise_g(G_RIGHT2 + 16, G_ALL)
                for v in range(1, 4):
                    move_plane(v, G_RIGHT2, G_ALL)
            if c == 10:
                copy_halo("s", 2, G_OWN, -1)
            if c == 11:
                quantise_g(0, 4)
                quantise_g(4, G_OWN)
                for v in range(1, 4):
                    move_plane(v, v, G_OWN)
        quantise_w(last, "s")
        for l in range(4, 10):
            mx(l, 0)
        for l in range(4, 10):
            mx(l, 1)

        o_sb = keep.tile([P, 8, P], F32, name="o_sb")
        res = keep.tile([P, 8, P], F32, name="res")
        o_view = o_sb[:].rearrange("p r (s a) -> p r s a", s=NS, a=8)

        def gather(k, r0, r1):
            nc.vector.tensor_copy(
                out=o_view[:, r0:r1, :, 4 * k:4 * k + 4],
                in_=acc[k][:].rearrange("p (a r s) -> p r s a", a=4, r=8, s=NS)[:, r0:r1])

        gather(0, 0, 8)
        for i in range(4):
            gather(1, 2 * i, 2 * i + 2)
        ots = [psum.tile([P, 2, P], F32, name="ot%d" % i, tag=XT_BANKS[i][0]) for i in range(4)]
        for i in range(4):
            for j in range(2):
                nc.tensor.transpose(ots[i][:, j, :], o_sb[:, 2 * i + j, :], ident[:])
        for eng, pieces in [("s", [0, 2]), ("v", [1, 3])]:
            for i in pieces:
                copy(eng, res[:, 2 * i:2 * i + 2, :], ots[i][:])
        for i in range(4):
            nc.sync.dma_start(out=out_view[:, 2 * i:2 * i + 2, :], in_=res[:, 2 * i:2 * i + 2, :])
